import numpy as np
import ml_dtypes

BF16 = ml_dtypes.bfloat16


def bf(x):
    return np.asarray(x, np.float32).astype(BF16)


def f32(x):
    return np.asarray(x, np.float32)


def f64(x):
    return np.asarray(x).astype(np.float64)


def striped(idx):
    return np.tile(idx.reshape(-1, 16).T, (8, 1))


E, C, S, N, M = 128, 256, 2048, 512, 512


def unit_columns(a):
    return a / np.sqrt(np.sum(a * a, axis=0, keepdims=True))


def setup_inputs():
    return {"rel": f32(np.random.standard_normal((C, S))), "head": f32(unit_columns(np.random.standard_normal((E, N)))), "tail": f32(unit_columns(np.random.standard_normal((E, M)))), "offs": striped(np.random.permutation(np.tile(np.arange(S), 2))[:N])}


def reference(rel, head, tail, offs):
    idx = offs[:16].T.reshape(-1)
    picked = f64(rel)[:, idx]
    u = picked[:E] * f64(head)
    rt = picked[E:]
    t = f64(tail)
    q = (t * t).T @ (rt * rt) - 2.0 * (t.T @ (rt * u)) + np.sum(u * u, axis=0)[None, :]
    return -np.sqrt(q)

@@ -1,0 +1,66 @@
+import concourse.mybir as mybir
+
+E = 128
+S = 2048
+N = 512
+M = 512
+P = 128
+
+F32 = mybir.dt.float32
+BF16 = mybir.dt.bfloat16
+U16 = mybir.dt.uint16
+MULT = mybir.AluOpType.mult
+ACT = mybir.ActivationFunctionType
+
+FLOPS = 3 * 2 * E * M * N
+
+
+def tile_pairre_kernel(tc, rel, head, tail, offs, out):
+    nc = tc.nc
+    with (
+        tc.tile_pool(name="held", bufs=1) as held,
+        tc.tile_pool(name="rows", bufs=2) as rows,
+        tc.psum_pool(name="psum", bufs=4) as psum,
+    ):
+        offsets = held.tile([P, N // 16], U16, name="offsets")
+        nc.sync.dma_start(offsets[:], offs)
+        head_sb = held.tile([E, N], F32, name="head_sb")
+        nc.sync.dma_start(head_sb[:], head)
+        rel_head = held.tile([E, S], F32, name="rel_head")
+        nc.sync.dma_start(rel_head[:], rel[0:E, :])
+        rel_tail = held.tile([E, S], F32, name="rel_tail")
+        nc.sync.dma_start(rel_tail[:], rel[E : 2 * E, :])
+        tail_sb = held.tile([E, M], F32, name="tail_sb")
+        nc.sync.dma_start(tail_sb[:], tail)
+
+        u = held.tile([E, N], F32, name="u")
+        nc.vector.tensor_tensor(u[:], rel_head[:].indirect(offsets[:]), head_sb[:], MULT)
+        rt_u = held.tile([E, N], F32, name="rt_u")
+        nc.vector.tensor_tensor(rt_u[:], rel_tail[:].indirect(offsets[:]), u[:], MULT)
+        rt = held.tile([E, N], F32, name="rt")
+        nc.vector.tensor_copy(rt[:], rel_tail[:].indirect(offsets[:]))
+
+        u_sq = held.tile([E, N], BF16, name="u_sq")
+        nc.scalar.activation(u_sq[:], u[:], ACT.Square)
+        rt_u_bf = held.tile([E, N], BF16, name="rt_u_bf")
+        nc.scalar.copy(rt_u_bf[:], rt_u[:])
+        rt_sq = held.tile([E, N], BF16, name="rt_sq")
+        nc.scalar.activation(rt_sq[:], rt[:], ACT.Square)
+        tail_sq = held.tile([E, M], BF16, name="tail_sq")
+        nc.scalar.activation(tail_sq[:], tail_sb[:], ACT.Square)
+        tail_m2 = held.tile([E, M], BF16, name="tail_m2")
+        nc.scalar.mul(tail_m2[:], tail_sb[:], -2.0)
+        ones = held.tile([E, P], BF16, name="ones")
+        nc.vector.memset(ones[:], 1.0)
+
+        for b in range(M // P):
+            block = slice(b * P, (b + 1) * P)
+            q = psum.tile([P, N], F32, name="q")
+            nc.tensor.matmul(q[:], ones[:], u_sq[:], start=True, stop=False)
+            nc.tensor.matmul(q[:], tail_m2[:, block], rt_u_bf[:], start=False, stop=False)
+            nc.tensor.matmul(q[:], tail_sq[:, block], rt_sq[:], start=False, stop=True)
+            root = rows.tile([P, N], F32, name="root")
+            nc.scalar.activation(root[:], q[:], ACT.Sqrt)
+            score = rows.tile([P, N], F32, name="score")
+            nc.vector.tensor_scalar_mul(score[:], root[:], -1.0)
+            nc.sync.dma_start(out[block, :], score[:])

@@ -5,6 +5,9 @@ S = 2048
 N = 512
 M = 512
 P = 128
+BLOCKS = M // P
+PIECES = 2
+W = N // PIECES
 
 F32 = mybir.dt.float32
 BF16 = mybir.dt.bfloat16
@@ -19,8 +22,7 @@ def tile_pairre_kernel(tc, rel, head, tail, offs, out):
     nc = tc.nc
     with (
         tc.tile_pool(name="held", bufs=1) as held,
-        tc.tile_pool(name="rows", bufs=2) as rows,
-        tc.psum_pool(name="psum", bufs=4) as psum,
+        tc.psum_pool(name="psum", bufs=PIECES * BLOCKS) as psum,
     ):
         offsets = held.tile([P, N // 16], U16, name="offsets")
         nc.sync.dma_start(offsets[:], offs)
@@ -33,34 +35,47 @@ def tile_pairre_kernel(tc, rel, head, tail, offs, out):
         tail_sb = held.tile([E, M], F32, name="tail_sb")
         nc.sync.dma_start(tail_sb[:], tail)
 
+        warm = held.tile([P, 1], F32, name="warm")
+        nc.gpsimd.memset(warm[:], 1.0)
+        nc.scalar.activation(warm[:], warm[:], ACT.Sqrt)
+        ones = held.tile([E, P], BF16, name="ones")
+        nc.gpsimd.memset(ones[:], 1.0)
+
         u = held.tile([E, N], F32, name="u")
         nc.vector.tensor_tensor(u[:], rel_head[:].indirect(offsets[:]), head_sb[:], MULT)
-        rt_u = held.tile([E, N], F32, name="rt_u")
-        nc.vector.tensor_tensor(rt_u[:], rel_tail[:].indirect(offsets[:]), u[:], MULT)
-        rt = held.tile([E, N], F32, name="rt")
-        nc.vector.tensor_copy(rt[:], rel_tail[:].indirect(offsets[:]))
-
         u_sq = held.tile([E, N], BF16, name="u_sq")
         nc.scalar.activation(u_sq[:], u[:], ACT.Square)
-        rt_u_bf = held.tile([E, N], BF16, name="rt_u_bf")
-        nc.scalar.copy(rt_u_bf[:], rt_u[:])
-        rt_sq = held.tile([E, N], BF16, name="rt_sq")
-        nc.scalar.activation(rt_sq[:], rt[:], ACT.Square)
+
+        q = [[psum.tile([P, W], F32, name="q") for b in range(BLOCKS)] for h in range(PIECES)]
+        for h in range(PIECES):
+            for b in range(BLOCKS):
+                nc.tensor.matmul(q[h][b][:], ones[:], u_sq[:, h * W : (h + 1) * W], start=True, stop=False)
+
         tail_sq = held.tile([E, M], BF16, name="tail_sq")
         nc.scalar.activation(tail_sq[:], tail_sb[:], ACT.Square)
         tail_m2 = held.tile([E, M], BF16, name="tail_m2")
-        nc.scalar.mul(tail_m2[:], tail_sb[:], -2.0)
-        ones = held.tile([E, P], BF16, name="ones")
-        nc.vector.memset(ones[:], 1.0)
+        nc.gpsimd.tensor_scalar_mul(tail_m2[:], tail_sb[:], -2.0)
 
-        for b in range(M // P):
-            block = slice(b * P, (b + 1) * P)
-            q = psum.tile([P, N], F32, name="q")
-            nc.tensor.matmul(q[:], ones[:], u_sq[:], start=True, stop=False)
-            nc.tensor.matmul(q[:], tail_m2[:, block], rt_u_bf[:], start=False, stop=False)
-            nc.tensor.matmul(q[:], tail_sq[:, block], rt_sq[:], start=False, stop=True)
-            root = rows.tile([P, N], F32, name="root")
-            nc.scalar.activation(root[:], q[:], ACT.Sqrt)
-            score = rows.tile([P, N], F32, name="score")
-            nc.vector.tensor_scalar_mul(score[:], root[:], -1.0)
-            nc.sync.dma_start(out[block, :], score[:])
+        rt_sq = []
+        rt_u_bf = []
+        for h in range(PIECES):
+            piece = offsets[:, h * (W // 16) : (h + 1) * (W // 16)]
+            rt = held.tile([E, W], F32, name=f"rt{h}")
+            nc.vector.tensor_copy(rt[:], rel_tail[:].indirect(piece))
+            rt_sq.append(held.tile([E, W], BF16, name=f"rt_sq{h}"))
+            nc.scalar.activation(rt_sq[h][:], rt[:], ACT.Square)
+            rt_u = held.tile([E, W], F32, name=f"rt_u{h}")
+            nc.vector.tensor_tensor(rt_u[:], rel_tail[:].indirect(piece), u[:, h * W : (h + 1) * W], MULT)
+            rt_u_bf.append(held.tile([E, W], BF16, name=f"rt_u_bf{h}"))
+            nc.vector.tensor_copy(rt_u_bf[h][:], rt_u[:])
+
+        for h in range(PIECES):
+            for b in range(BLOCKS):
+                block = slice(b * P, (b + 1) * P)
+                nc.tensor.matmul(q[h][b][:], tail_sq[:, block], rt_sq[h][:], start=False, stop=False)
+                nc.tensor.matmul(q[h][b][:], tail_m2[:, block], rt_u_bf[h][:], start=False, stop=True)
+                root = held.tile([P, W], F32, name=f"root{h}{b}")
+                nc.scalar.activation(root[:], q[h][b][:], ACT.Sqrt)
+                score = held.tile([P, W], F32, name=f"score{h}{b}")
+                nc.vector.tensor_scalar_mul(score[:], root[:], -1.0)
+                nc.sync.dma_start(out[block, h * W : (h + 1) * W], score[:])

@@ -26,20 +26,25 @@ def tile_pairre_kernel(tc, rel, head, tail, offs, out):
     ):
         offsets = held.tile([P, N // 16], U16, name="offsets")
         nc.sync.dma_start(offsets[:], offs)
+        tail_sb = held.tile([E, M], F32, name="tail_sb")
+        nc.sync.dma_start(tail_sb[:], tail)
         head_sb = held.tile([E, N], F32, name="head_sb")
         nc.sync.dma_start(head_sb[:], head)
         rel_head = held.tile([E, S], F32, name="rel_head")
         nc.sync.dma_start(rel_head[:], rel[0:E, :])
         rel_tail = held.tile([E, S], F32, name="rel_tail")
         nc.sync.dma_start(rel_tail[:], rel[E : 2 * E, :])
-        tail_sb = held.tile([E, M], F32, name="tail_sb")
-        nc.sync.dma_start(tail_sb[:], tail)
 
         warm = held.tile([P, 1], F32, name="warm")
         nc.gpsimd.memset(warm[:], 1.0)
         nc.scalar.activation(warm[:], warm[:], ACT.Sqrt)
         ones = held.tile([E, P], BF16, name="ones")
         nc.gpsimd.memset(ones[:], 1.0)
+
+        tail_sq = held.tile([E, M], BF16, name="tail_sq")
+        nc.scalar.activation(tail_sq[:], tail_sb[:], ACT.Square)
+        tail_m2 = held.tile([E, M], BF16, name="tail_m2")
+        nc.scalar.mul(tail_m2[:], tail_sb[:], -2.0)
 
         u = held.tile([E, N], F32, name="u")
         nc.vector.tensor_tensor(u[:], rel_head[:].indirect(offsets[:]), head_sb[:], MULT)
@@ -50,11 +55,6 @@ def tile_pairre_kernel(tc, rel, head, tail, offs, out):
         for h in range(PIECES):
             for b in range(BLOCKS):
                 nc.tensor.matmul(q[h][b][:], ones[:], u_sq[:, h * W : (h + 1) * W], start=True, stop=False)
-
-        tail_sq = held.tile([E, M], BF16, name="tail_sq")
-        nc.scalar.activation(tail_sq[:], tail_sb[:], ACT.Square)
-        tail_m2 = held.tile([E, M], BF16, name="tail_m2")
-        nc.gpsimd.tensor_scalar_mul(tail_m2[:], tail_sb[:], -2.0)
 
         rt_sq = []
         rt_u_bf = []

@@ -8,6 +8,7 @@ P = 128
 BLOCKS = M // P
 PIECES = 2
 W = N // PIECES
+WARM_MATMULS = 32
 
 F32 = mybir.dt.float32
 BF16 = mybir.dt.bfloat16
@@ -38,8 +39,12 @@ def tile_pairre_kernel(tc, rel, head, tail, offs, out):
         warm = held.tile([P, 1], F32, name="warm")
         nc.gpsimd.memset(warm[:], 1.0)
         nc.scalar.activation(warm[:], warm[:], ACT.Sqrt)
-        ones = held.tile([E, P], BF16, name="ones")
+        ones = held.tile([E, W], BF16, name="ones")
         nc.gpsimd.memset(ones[:], 1.0)
+
+        q = [[psum.tile([P, W], F32, name="q") for b in range(BLOCKS)] for h in range(PIECES)]
+        for i in range(WARM_MATMULS):
+            nc.tensor.matmul(q[PIECES - 1][BLOCKS - 1][:], ones[:, 0:P], ones[:], start=True, stop=True)
 
         tail_sq = held.tile([E, M], BF16, name="tail_sq")
         nc.scalar.activation(tail_sq[:], tail_sb[:], ACT.Square)
@@ -51,10 +56,9 @@ def tile_pairre_kernel(tc, rel, head, tail, offs, out):
         u_sq = held.tile([E, N], BF16, name="u_sq")
         nc.scalar.activation(u_sq[:], u[:], ACT.Square)
 
-        q = [[psum.tile([P, W], F32, name="q") for b in range(BLOCKS)] for h in range(PIECES)]
         for h in range(PIECES):
             for b in range(BLOCKS):
-                nc.tensor.matmul(q[h][b][:], ones[:], u_sq[:, h * W : (h + 1) * W], start=True, stop=False)
+                nc.tensor.matmul(q[h][b][:], ones[:, 0:P], u_sq[:, h * W : (h + 1) * W], start=True, stop=False)
 
         rt_sq = []
         rt_u_bf = []

@@ -8,15 +8,16 @@ P = 128
 BLOCKS = M // P
 PIECES = 2
 W = N // PIECES
-WARM_MATMULS = 32
 
 F32 = mybir.dt.float32
 BF16 = mybir.dt.bfloat16
 U16 = mybir.dt.uint16
 MULT = mybir.AluOpType.mult
+MIN = mybir.AluOpType.min
 ACT = mybir.ActivationFunctionType
 
 FLOPS = 3 * 2 * E * M * N
+TINY = 1.0e-26
 
 
 def tile_pairre_kernel(tc, rel, head, tail, offs, out):
@@ -36,29 +37,27 @@ def tile_pairre_kernel(tc, rel, head, tail, offs, out):
         rel_tail = held.tile([E, S], F32, name="rel_tail")
         nc.sync.dma_start(rel_tail[:], rel[E : 2 * E, :])
 
+        neg_tiny = held.tile([P, 1], F32, name="neg_tiny")
+        nc.gpsimd.memset(neg_tiny[:], -TINY)
         warm = held.tile([P, 1], F32, name="warm")
-        nc.gpsimd.memset(warm[:], 1.0)
-        nc.scalar.activation(warm[:], warm[:], ACT.Sqrt)
-        ones = held.tile([E, W], BF16, name="ones")
-        nc.gpsimd.memset(ones[:], 1.0)
+        nc.scalar.activation(warm[:], neg_tiny[:], ACT.Abs_reciprocal_sqrt)
+        neg_ones = held.tile([E, P], BF16, name="neg_ones")
+        nc.gpsimd.memset(neg_ones[:], -1.0)
 
-        q = [[psum.tile([P, W], F32, name="q") for b in range(BLOCKS)] for h in range(PIECES)]
-        for i in range(WARM_MATMULS):
-            nc.tensor.matmul(q[PIECES - 1][BLOCKS - 1][:], ones[:, 0:P], ones[:], start=True, stop=True)
-
-        tail_sq = held.tile([E, M], BF16, name="tail_sq")
-        nc.scalar.activation(tail_sq[:], tail_sb[:], ACT.Square)
-        tail_m2 = held.tile([E, M], BF16, name="tail_m2")
-        nc.scalar.mul(tail_m2[:], tail_sb[:], -2.0)
+        neg_tail_sq = held.tile([E, M], BF16, name="neg_tail_sq")
+        nc.vector.scalar_tensor_tensor(neg_tail_sq[:], tail_sb[:], -1.0, tail_sb[:], MULT, MULT)
+        tail_x2 = held.tile([E, M], BF16, name="tail_x2")
+        nc.scalar.mul(tail_x2[:], tail_sb[:], 2.0)
 
         u = held.tile([E, N], F32, name="u")
         nc.vector.tensor_tensor(u[:], rel_head[:].indirect(offsets[:]), head_sb[:], MULT)
         u_sq = held.tile([E, N], BF16, name="u_sq")
         nc.scalar.activation(u_sq[:], u[:], ACT.Square)
 
+        neg_q = [[psum.tile([P, W], F32, name="neg_q") for b in range(BLOCKS)] for h in range(PIECES)]
         for h in range(PIECES):
             for b in range(BLOCKS):
-                nc.tensor.matmul(q[h][b][:], ones[:, 0:P], u_sq[:, h * W : (h + 1) * W], start=True, stop=False)
+                nc.tensor.matmul(neg_q[h][b][:], neg_ones[:], u_sq[:, h * W : (h + 1) * W], start=True, stop=False)
 
         rt_sq = []
         rt_u_bf = []
@@ -76,10 +75,10 @@ def tile_pairre_kernel(tc, rel, head, tail, offs, out):
         for h in range(PIECES):
             for b in range(BLOCKS):
                 block = slice(b * P, (b + 1) * P)
-                nc.tensor.matmul(q[h][b][:], tail_sq[:, block], rt_sq[h][:], start=False, stop=False)
-                nc.tensor.matmul(q[h][b][:], tail_m2[:, block], rt_u_bf[h][:], start=False, stop=True)
-                root = held.tile([P, W], F32, name=f"root{h}{b}")
-                nc.scalar.activation(root[:], q[h][b][:], ACT.Sqrt)
+                nc.tensor.matmul(neg_q[h][b][:], neg_tail_sq[:, block], rt_sq[h][:], start=False, stop=False)
+                nc.tensor.matmul(neg_q[h][b][:], tail_x2[:, block], rt_u_bf[h][:], start=False, stop=True)
+                inv_root = held.tile([P, W], F32, name=f"inv_root{h}{b}")
+                nc.scalar.activation(inv_root[:], neg_q[h][b][:], ACT.Abs_reciprocal_sqrt, bias=neg_tiny[:])
                 score = held.tile([P, W], F32, name=f"score{h}{b}")
-                nc.vector.tensor_scalar_mul(score[:], root[:], -1.0)
+                nc.vector.scalar_tensor_tensor(score[:], neg_q[h][b][:], 0.0, inv_root[:], MIN, MULT)
                 nc.sync.dma_start(out[block, h * W : (h + 1) * W], score[:])

@@ -70,7 +70,7 @@ def tile_pairre_kernel(tc, rel, head, tail, offs, out):
             rt_u = held.tile([E, W], F32, name=f"rt_u{h}")
             nc.vector.tensor_tensor(rt_u[:], rel_tail[:].indirect(piece), u[:, h * W : (h + 1) * W], MULT)
             rt_u_bf.append(held.tile([E, W], BF16, name=f"rt_u_bf{h}"))
-            nc.vector.tensor_copy(rt_u_bf[h][:], rt_u[:])
+            nc.scalar.copy(rt_u_bf[h][:], rt_u[:])
 
         for h in range(PIECES):
             for b in range(BLOCKS):

@@ -49,15 +49,16 @@ def tile_pairre_kernel(tc, rel, head, tail, offs, out):
         tail_x2 = held.tile([E, M], BF16, name="tail_x2")
         nc.scalar.mul(tail_x2[:], tail_sb[:], 2.0)
 
-        u = held.tile([E, N], F32, name="u")
-        nc.vector.tensor_tensor(u[:], rel_head[:].indirect(offsets[:]), head_sb[:], MULT)
-        u_sq = held.tile([E, N], BF16, name="u_sq")
-        nc.scalar.activation(u_sq[:], u[:], ACT.Square)
-
+        u = []
         neg_q = [[psum.tile([P, W], F32, name="neg_q") for b in range(BLOCKS)] for h in range(PIECES)]
         for h in range(PIECES):
+            piece = offsets[:, h * (W // 16) : (h + 1) * (W // 16)]
+            u.append(held.tile([E, W], F32, name=f"u{h}"))
+            nc.vector.tensor_tensor(u[h][:], rel_head[:].indirect(piece), head_sb[:, h * W : (h + 1) * W], MULT)
+            u_sq = held.tile([E, W], BF16, name=f"u_sq{h}")
+            nc.scalar.activation(u_sq[:], u[h][:], ACT.Square)
             for b in range(BLOCKS):
-                nc.tensor.matmul(neg_q[h][b][:], neg_ones[:], u_sq[:, h * W : (h + 1) * W], start=True, stop=False)
+                nc.tensor.matmul(neg_q[h][b][:], neg_ones[:], u_sq[:], start=True, stop=False)
 
         rt_sq = []
         rt_u_bf = []
@@ -68,7 +69,7 @@ def tile_pairre_kernel(tc, rel, head, tail, offs, out):
             rt_sq.append(held.tile([E, W], BF16, name=f"rt_sq{h}"))
             nc.scalar.activation(rt_sq[h][:], rt[:], ACT.Square)
             rt_u = held.tile([E, W], F32, name=f"rt_u{h}")
-            nc.vector.tensor_tensor(rt_u[:], rel_tail[:].indirect(piece), u[:, h * W : (h + 1) * W], MULT)
+            nc.vector.tensor_tensor(rt_u[:], rel_tail[:].indirect(piece), u[h][:], MULT)
             rt_u_bf.append(held.tile([E, W], BF16, name=f"rt_u_bf{h}"))
             nc.scalar.copy(rt_u_bf[h][:], rt_u[:])
 

@@ -13,7 +13,6 @@ F32 = mybir.dt.float32
 BF16 = mybir.dt.bfloat16
 U16 = mybir.dt.uint16
 MULT = mybir.AluOpType.mult
-MIN = mybir.AluOpType.min
 ACT = mybir.ActivationFunctionType
 
 FLOPS = 3 * 2 * E * M * N
@@ -28,29 +27,24 @@ def tile_pairre_kernel(tc, rel, head, tail, offs, out):
     ):
         offsets = held.tile([P, N // 16], U16, name="offsets")
         nc.sync.dma_start(offsets[:], offs)
-        tail_sb = held.tile([E, M], F32, name="tail_sb")
-        nc.sync.dma_start(tail_sb[:], tail)
         head_sb = held.tile([E, N], F32, name="head_sb")
         nc.sync.dma_start(head_sb[:], head)
         rel_head = held.tile([E, S], F32, name="rel_head")
         nc.sync.dma_start(rel_head[:], rel[0:E, :])
         rel_tail = held.tile([E, S], F32, name="rel_tail")
         nc.sync.dma_start(rel_tail[:], rel[E : 2 * E, :])
+        tail_sb = held.tile([E, M], F32, name="tail_sb")
+        nc.sync.dma_start(tail_sb[:], tail)
 
-        neg_tiny = held.tile([P, 1], F32, name="neg_tiny")
-        nc.gpsimd.memset(neg_tiny[:], -TINY)
+        tiny = held.tile([P, 1], F32, name="tiny")
+        nc.gpsimd.memset(tiny[:], TINY)
         warm = held.tile([P, 1], F32, name="warm")
-        nc.scalar.activation(warm[:], neg_tiny[:], ACT.Abs_reciprocal_sqrt)
-        neg_ones = held.tile([E, P], BF16, name="neg_ones")
-        nc.gpsimd.memset(neg_ones[:], -1.0)
-
-        neg_tail_sq = held.tile([E, M], BF16, name="neg_tail_sq")
-        nc.vector.scalar_tensor_tensor(neg_tail_sq[:], tail_sb[:], -1.0, tail_sb[:], MULT, MULT)
-        tail_x2 = held.tile([E, M], BF16, name="tail_x2")
-        nc.scalar.mul(tail_x2[:], tail_sb[:], 2.0)
+        nc.scalar.activation(warm[:], tiny[:], ACT.Abs_reciprocal_sqrt)
+        ones = held.tile([E, P], BF16, name="ones")
+        nc.gpsimd.memset(ones[:], 1.0)
 
         u = []
-        neg_q = [[psum.tile([P, W], F32, name="neg_q") for b in range(BLOCKS)] for h in range(PIECES)]
+        q = [[psum.tile([P, W], F32, name="q") for b in range(BLOCKS)] for h in range(PIECES)]
         for h in range(PIECES):
             piece = offsets[:, h * (W // 16) : (h + 1) * (W // 16)]
             u.append(held.tile([E, W], F32, name=f"u{h}"))
@@ -58,7 +52,14 @@ def tile_pairre_kernel(tc, rel, head, tail, offs, out):
             u_sq = held.tile([E, W], BF16, name=f"u_sq{h}")
             nc.scalar.activation(u_sq[:], u[h][:], ACT.Square)
             for b in range(BLOCKS):
-                nc.tensor.matmul(neg_q[h][b][:], neg_ones[:], u_sq[:], start=True, stop=False)
+                nc.tensor.matmul(q[h][b][:], ones[:], u_sq[:], start=True, stop=False)
+
+        tail_sq = held.tile([E, M], BF16, name="tail_sq")
+        tail_xm2 = held.tile([E, M], BF16, name="tail_xm2")
+        for b in range(BLOCKS):
+            block = slice(b * P, (b + 1) * P)
+            nc.scalar.activation(tail_sq[:, block], tail_sb[:, block], ACT.Square)
+            nc.scalar.mul(tail_xm2[:, block], tail_sb[:, block], -2.0)
 
         rt_sq = []
         rt_u_bf = []
@@ -71,15 +72,15 @@ def tile_pairre_kernel(tc, rel, head, tail, offs, out):
             rt_u = held.tile([E, W], F32, name=f"rt_u{h}")
             nc.vector.tensor_tensor(rt_u[:], rel_tail[:].indirect(piece), u[h][:], MULT)
             rt_u_bf.append(held.tile([E, W], BF16, name=f"rt_u_bf{h}"))
-            nc.scalar.copy(rt_u_bf[h][:], rt_u[:])
+            nc.vector.tensor_copy(rt_u_bf[h][:], rt_u[:])
 
         for h in range(PIECES):
             for b in range(BLOCKS):
                 block = slice(b * P, (b + 1) * P)
-                nc.tensor.matmul(neg_q[h][b][:], neg_tail_sq[:, block], rt_sq[h][:], start=False, stop=False)
-                nc.tensor.matmul(neg_q[h][b][:], tail_x2[:, block], rt_u_bf[h][:], start=False, stop=True)
+                nc.tensor.matmul(q[h][b][:], tail_sq[:, block], rt_sq[h][:], start=False, stop=False)
+                nc.tensor.matmul(q[h][b][:], tail_xm2[:, block], rt_u_bf[h][:], start=False, stop=True)
                 inv_root = held.tile([P, W], F32, name=f"inv_root{h}{b}")
-                nc.scalar.activation(inv_root[:], neg_q[h][b][:], ACT.Abs_reciprocal_sqrt, bias=neg_tiny[:])
+                nc.scalar.activation(inv_root[:], q[h][b][:], ACT.Abs_reciprocal_sqrt, bias=tiny[:])
                 score = held.tile([P, W], F32, name=f"score{h}{b}")
-                nc.vector.scalar_tensor_tensor(score[:], neg_q[h][b][:], 0.0, inv_root[:], MIN, MULT)
+                nc.vector.scalar_tensor_tensor(score[:], q[h][b][:], -1.0, inv_root[:], MULT, MULT)
                 nc.sync.dma_start(out[block, h * W : (h + 1) * W], score[:])

@@ -55,11 +55,9 @@ def tile_pairre_kernel(tc, rel, head, tail, offs, out):
                 nc.tensor.matmul(q[h][b][:], ones[:], u_sq[:], start=True, stop=False)
 
         tail_sq = held.tile([E, M], BF16, name="tail_sq")
+        nc.scalar.activation(tail_sq[:], tail_sb[:], ACT.Square)
         tail_xm2 = held.tile([E, M], BF16, name="tail_xm2")
-        for b in range(BLOCKS):
-            block = slice(b * P, (b + 1) * P)
-            nc.scalar.activation(tail_sq[:, block], tail_sb[:, block], ACT.Square)
-            nc.scalar.mul(tail_xm2[:, block], tail_sb[:, block], -2.0)
+        nc.scalar.mul(tail_xm2[:], tail_sb[:], -2.0)
 
         rt_sq = []
         rt_u_bf = []
@@ -72,7 +70,7 @@ def tile_pairre_kernel(tc, rel, head, tail, offs, out):
             rt_u = held.tile([E, W], F32, name=f"rt_u{h}")
             nc.vector.tensor_tensor(rt_u[:], rel_tail[:].indirect(piece), u[h][:], MULT)
             rt_u_bf.append(held.tile([E, W], BF16, name=f"rt_u_bf{h}"))
-            nc.vector.tensor_copy(rt_u_bf[h][:], rt_u[:])
+            nc.scalar.copy(rt_u_bf[h][:], rt_u[:])
 
         for h in range(PIECES):
             for b in range(BLOCKS):

@@ -37,11 +37,11 @@ def tile_pairre_kernel(tc, rel, head, tail, offs, out):
         nc.sync.dma_start(tail_sb[:], tail)
 
         tiny = held.tile([P, 1], F32, name="tiny")
-        nc.gpsimd.memset(tiny[:], TINY)
+        nc.vector.memset(tiny[:], TINY)
         warm = held.tile([P, 1], F32, name="warm")
         nc.scalar.activation(warm[:], tiny[:], ACT.Abs_reciprocal_sqrt)
         ones = held.tile([E, P], BF16, name="ones")
-        nc.gpsimd.memset(ones[:], 1.0)
+        nc.vector.memset(ones[:], 1.0)
 
         u = []
         q = [[psum.tile([P, W], F32, name="q") for b in range(BLOCKS)] for h in range(PIECES)]

@@ -66,11 +66,11 @@ def tile_pairre_kernel(tc, rel, head, tail, offs, out):
             rt = held.tile([E, W], F32, name=f"rt{h}")
             nc.vector.tensor_copy(rt[:], rel_tail[:].indirect(piece))
             rt_sq.append(held.tile([E, W], BF16, name=f"rt_sq{h}"))
-            nc.scalar.activation(rt_sq[h][:], rt[:], ACT.Square)
+            nc.vector.tensor_tensor(rt_sq[h][:], rt[:], rt[:], MULT)
             rt_u = held.tile([E, W], F32, name=f"rt_u{h}")
             nc.vector.tensor_tensor(rt_u[:], rel_tail[:].indirect(piece), u[h][:], MULT)
             rt_u_bf.append(held.tile([E, W], BF16, name=f"rt_u_bf{h}"))
-            nc.scalar.copy(rt_u_bf[h][:], rt_u[:])
+            nc.vector.tensor_copy(rt_u_bf[h][:], rt_u[:])
 
         for h in range(PIECES):
             for b in range(BLOCKS):

import concourse.mybir as mybir

E = 128
S = 2048
N = 512
M = 512
P = 128
BLOCKS = M // P
PIECES = 2
W = N // PIECES

F32 = mybir.dt.float32
BF16 = mybir.dt.bfloat16
U16 = mybir.dt.uint16
MULT = mybir.AluOpType.mult
ACT = mybir.ActivationFunctionType

FLOPS = 3 * 2 * E * M * N
TINY = 1.0e-26


def tile_pairre_kernel(tc, rel, head, tail, offs, out):
    nc = tc.nc
    with (
        tc.tile_pool(name="held", bufs=1) as held,
        tc.psum_pool(name="psum", bufs=PIECES * BLOCKS) as psum,
    ):
        offsets = held.tile([P, N // 16], U16, name="offsets")
        nc.sync.dma_start(offsets[:], offs)
        head_sb = held.tile([E, N], F32, name="head_sb")
        nc.sync.dma_start(head_sb[:], head)
        rel_head = held.tile([E, S], F32, name="rel_head")
        nc.sync.dma_start(rel_head[:], rel[0:E, :])
        rel_tail = held.tile([E, S], F32, name="rel_tail")
        nc.sync.dma_start(rel_tail[:], rel[E : 2 * E, :])
        tail_sb = held.tile([E, M], F32, name="tail_sb")
        nc.sync.dma_start(tail_sb[:], tail)

        tiny = held.tile([P, 1], F32, name="tiny")
        nc.vector.memset(tiny[:], TINY)
        warm = held.tile([P, 1], F32, name="warm")
        nc.scalar.activation(warm[:], tiny[:], ACT.Abs_reciprocal_sqrt)
        ones = held.tile([E, P], BF16, name="ones")
        nc.vector.memset(ones[:], 1.0)

        u = []
        q = [[psum.tile([P, W], F32, name="q") for b in range(BLOCKS)] for h in range(PIECES)]
        for h in range(PIECES):
            piece = offsets[:, h * (W // 16) : (h + 1) * (W // 16)]
            u.append(held.tile([E, W], F32, name=f"u{h}"))
            nc.vector.tensor_tensor(u[h][:], rel_head[:].indirect(piece), head_sb[:, h * W : (h + 1) * W], MULT)
            u_sq = held.tile([E, W], BF16, name=f"u_sq{h}")
            nc.scalar.activation(u_sq[:], u[h][:], ACT.Square)
            for b in range(BLOCKS):
                nc.tensor.matmul(q[h][b][:], ones[:], u_sq[:], start=True, stop=False)

        tail_sq = held.tile([E, M], BF16, name="tail_sq")
        nc.scalar.activation(tail_sq[:], tail_sb[:], ACT.Square)
        tail_xm2 = held.tile([E, M], BF16, name="tail_xm2")
        nc.scalar.mul(tail_xm2[:], tail_sb[:], -2.0)

        rt_sq = []
        rt_u_bf = []
        for h in range(PIECES):
            piece = offsets[:, h * (W // 16) : (h + 1) * (W // 16)]
            rt = held.tile([E, W], F32, name=f"rt{h}")
            nc.vector.tensor_copy(rt[:], rel_tail[:].indirect(piece))
            rt_sq.append(held.tile([E, W], BF16, name=f"rt_sq{h}"))
            nc.vector.tensor_tensor(rt_sq[h][:], rt[:], rt[:], MULT)
            rt_u = held.tile([E, W], F32, name=f"rt_u{h}")
            nc.vector.tensor_tensor(rt_u[:], rel_tail[:].indirect(piece), u[h][:], MULT)
            rt_u_bf.append(held.tile([E, W], BF16, name=f"rt_u_bf{h}"))
            nc.vector.tensor_copy(rt_u_bf[h][:], rt_u[:])

        for h in range(PIECES):
            for b in range(BLOCKS):
                block = slice(b * P, (b + 1) * P)
                nc.tensor.matmul(q[h][b][:], tail_sq[:, block], rt_sq[h][:], start=False, stop=False)
                nc.tensor.matmul(q[h][b][:], tail_xm2[:, block], rt_u_bf[h][:], start=False, stop=True)
                inv_root = held.tile([P, W], F32, name=f"inv_root{h}{b}")
                nc.scalar.activation(inv_root[:], q[h][b][:], ACT.Abs_reciprocal_sqrt, bias=tiny[:])
                score = held.tile([P, W], F32, name=f"score{h}{b}")
                nc.vector.scalar_tensor_tensor(score[:], q[h][b][:], -1.0, inv_root[:], MULT, MULT)
                nc.sync.dma_start(out[block, h * W : (h + 1) * W], score[:])
